import numpy as np
import ml_dtypes


def mxq(x, axis, fmt="e4m3"):
    dtype, down = {"e4m3": (ml_dtypes.float8_e4m3fn, 7), "e5m2": (ml_dtypes.float8_e5m2, 14)}[fmt]
    v = np.moveaxis(np.asarray(x, np.float32).astype(ml_dtypes.bfloat16).astype(np.float64), axis, -1)
    blocks = v.reshape(v.shape[:-1] + (-1, 32))
    amax = np.abs(blocks).max(-1, keepdims=True)
    byte = np.maximum(np.where(amax > 0, np.frexp(amax)[1] - 1 + 127, 0) - down, 1)
    scale = np.exp2(byte - 127.0)
    codes = (blocks / scale).astype(np.float32).astype(dtype).astype(np.float64)
    return np.moveaxis((codes * scale).reshape(v.shape), -1, axis)


WIDE = False


def mx_kscale(k):
    if not WIDE:
        return np.ones(k)
    levels = np.array([10, -10, 5, -5, 0])
    a = np.random.permutation(np.resize(levels, k // 512 * 4)).reshape(k // 512, 4)
    idx = np.arange(k)
    return np.exp2(a[idx // 512, idx % 128 // 32])


BF16 = ml_dtypes.bfloat16


def bf(x):
    return np.asarray(x, np.float32).astype(BF16)


def f64(x):
    return np.asarray(x).astype(np.float64)


B, S, D, K = 512, 8, 1024, 512


def setup_inputs():
    t = np.exp2(np.round(np.log2(mx_kscale(D)) / 2))
    q = np.random.standard_normal((B, S, D))
    a = 0.3 * np.random.standard_normal((B, S, 1))
    p = np.random.standard_normal((B, S, D)) + a * q[:, -1:, :]
    W = np.random.uniform(0.0, 1.0, (K, D)) * np.sqrt(12.0 / D)
    return {"p": bf(p / t), "q": bf(q / t), "W": bf(W * t)}


def reference(p, q, W):
    p, q, W = f64(p), f64(q), f64(W)
    W2 = mxq(W * W, 1, "e4m3")
    q_last = q[:, -1, :]
    dot = (mxq(p * q_last[:, None, :], 2, "e4m3") @ W2.T).transpose(0, 2, 1)
    norm_p = np.sqrt((mxq(p * p, 2, "e4m3") @ W2.T).transpose(0, 2, 1))
    norm_q = np.sqrt(mxq(q_last * q_last, 1, "e4m3") @ W2.T)
    dist = -dot / (norm_p * norm_q[:, :, None] * D)
    return dist.reshape(B, S, -1)

@@ -1,0 +1,211 @@
+from contextlib import ExitStack
+
+import concourse.mybir as mybir
+from concourse.masks import make_identity
+
+F32 = mybir.dt.float32
+BF16 = mybir.dt.bfloat16
+U32 = mybir.dt.uint32
+U8 = mybir.dt.uint8
+FP8X4 = mybir.dt.float8_e4m3fn_x4
+FN = mybir.ActivationFunctionType
+ALU = mybir.AluOpType
+
+P = 128
+B, S, D, K = 512, 8, 1024, 512
+NBT = B // P
+NKT = K // P
+SH = 4
+ROUNDS = NBT * (S // SH)
+PASSES = D // 512
+WORDS = D // 4
+
+FLOPS = 2 * (2 * B * S + B) * K * D
+BYTES = 2 * (B * S * D + B * D + K * D) + 4 * B * S * K
+
+VECTOR_FINAL_KT = ()
+
+
+def tile_mpl_t_kernel(tc, p, q, W, out):
+    nc = tc.nc
+    out_flat = out.rearrange("b s k -> b (s k)")
+    with ExitStack() as ctx:
+        const = ctx.enter_context(tc.tile_pool(name="const", bufs=1))
+        loads = ctx.enter_context(tc.tile_pool(name="loads", bufs=8))
+        scratch = ctx.enter_context(tc.tile_pool(name="scratch", bufs=2))
+        prods = ctx.enter_context(tc.tile_pool(name="prods", bufs=2))
+        epi = ctx.enter_context(tc.tile_pool(name="epi", bufs=2))
+        outs = ctx.enter_context(tc.tile_pool(name="outs", bufs=2))
+        psx = ctx.enter_context(tc.psum_pool(name="psx", bufs=4))
+        psn = ctx.enter_context(tc.psum_pool(name="psn", bufs=2))
+        psd = ctx.enter_context(tc.psum_pool(name="psd", bufs=2))
+
+        ident = const.tile([P, P], F32, name="ident")
+        make_identity(nc, ident[:])
+
+        w_ld = loads.tile([P, NKT * D], BF16, name="ld")
+        for kt in range(NKT):
+            nc.sync.dma_start(out=w_ld[:, kt * D:(kt + 1) * D], in_=W[kt * P:(kt + 1) * P, :])
+        q_ld = loads.tile([P, NBT * D], BF16, name="ld")
+        for bt in range(NBT):
+            nc.sync.dma_start(out=q_ld[:, bt * D:(bt + 1) * D], in_=q[bt * P:(bt + 1) * P, S - 1, :])
+        p_ld = []
+        for r in range(ROUNDS):
+            bt, sh = divmod(r, S // SH)
+            ld = loads.tile([P, SH * D], BF16, name="ld")
+            nc.sync.dma_start(
+                out=ld[:],
+                in_=p[bt * P:(bt + 1) * P, sh * SH:(sh + 1) * SH, :].rearrange("b s d -> b (s d)"),
+            )
+            p_ld.append(ld)
+
+        def transpose_unit(src):
+            xt = psx.tile([P, 512], F32, name="xt")
+            words = src.bitcast(F32)
+            for g in range(PASSES):
+                for u in range(2):
+                    nc.tensor.transpose(
+                        out=xt[:, u * 256 + g * P:u * 256 + (g + 1) * P],
+                        in_=words[:, g * 256 + u * P:g * 256 + (u + 1) * P],
+                        identity=ident[:],
+                    )
+            return xt
+
+        def bank_values(xt):
+            return xt[:].bitcast(BF16).rearrange("p (u c e) -> p c u e", u=2, e=2)
+
+        def bank_words(xt):
+            return xt[:].rearrange("p (u c) -> p c u", u=2)
+
+        def grouped(ap):
+            return ap.rearrange("p (c u e) -> p c u e", u=2, e=2)
+
+        def quantise(src, codes, scales, first, count):
+            nc.vector.quantize_mx(
+                out=codes[:, first * WORDS:(first + count) * WORDS].bitcast(FP8X4),
+                scales=scales[:, first * WORDS:(first + count) * WORDS],
+                in_=src[:, first * D:(first + count) * D],
+            )
+
+        def mx_group(dst, a_codes, a_scales, a_unit, kt):
+            for g in range(PASSES):
+                a0 = a_unit * WORDS + g * P
+                w0 = kt * WORDS + g * P
+                nc.tensor.matmul_mx(
+                    out=dst,
+                    lhsT=a_codes[:, a0:a0 + P].bitcast(FP8X4),
+                    lhsT_scale=a_scales[:, a0:a0 + P],
+                    rhs=w_codes[:, w0:w0 + P].bitcast(FP8X4),
+                    rhs_scale=w_scales[:, w0:w0 + P],
+                    start=(g == 0),
+                    stop=(g == PASSES - 1),
+                )
+
+        w_sq = const.tile([P, NKT * D], BF16, name="w_sq", align_bytes=64)
+        w_codes = const.tile([P, NKT * WORDS], U32, name="w_codes", align_bytes=64)
+        w_scales = const.tile([P, NKT * WORDS], U8, name="w_scales", align_bytes=64)
+        for kt in range(NKT):
+            xt = transpose_unit(w_ld[:, kt * D:(kt + 1) * D])
+            dst = w_sq[:, kt * D:(kt + 1) * D]
+            if kt % 2 == 0:
+                nc.scalar.activation(out=grouped(dst), in_=bank_values(xt), func=FN.Square)
+            else:
+                raw = scratch.tile([P, D], BF16, name="raw")
+                nc.vector.tensor_copy(
+                    out=raw[:].bitcast(F32).rearrange("p (c u) -> p c u", u=2), in_=bank_words(xt)
+                )
+                nc.vector.tensor_tensor(out=dst, in0=raw[:], in1=raw[:], op=ALU.mult)
+            if kt % 2 == 1:
+                quantise(w_sq, w_codes, w_scales, kt - 1, 2)
+
+        q_raw = const.tile([P, NBT * D], BF16, name="q_raw")
+        q_sq = const.tile([P, NBT * D], BF16, name="q_sq", align_bytes=64)
+        q_codes = const.tile([P, NBT * WORDS], U32, name="q_codes", align_bytes=64)
+        q_scales = const.tile([P, NBT * WORDS], U8, name="q_scales", align_bytes=64)
+        for bt in range(NBT):
+            xt = transpose_unit(q_ld[:, bt * D:(bt + 1) * D])
+            nc.vector.tensor_copy(
+                out=q_raw[:, bt * D:(bt + 1) * D].bitcast(F32).rearrange("p (c u) -> p c u", u=2),
+                in_=bank_words(xt),
+            )
+            nc.scalar.activation(
+                out=grouped(q_sq[:, bt * D:(bt + 1) * D]), in_=bank_values(xt), func=FN.Square
+            )
+            if bt % 2 == 1:
+                quantise(q_sq, q_codes, q_scales, bt - 1, 2)
+
+        factor = const.tile([P, NBT * K], F32, name="factor")
+        for bt in range(NBT):
+            nq = psn.tile([P, K], F32, name="npb")
+            for kt in range(NKT):
+                mx_group(nq[:, kt * P:(kt + 1) * P], q_codes, q_scales, bt, kt)
+            f = factor[:, bt * K:(bt + 1) * K]
+            nc.scalar.activation(out=f, in_=nq[:], func=FN.Abs_reciprocal_sqrt)
+            nc.vector.tensor_scalar_mul(out=f, in0=f, scalar1=-1.0 / D)
+
+        state = {}
+
+        def front(r):
+            bt = r // (S // SH)
+            prod = prods.tile([P, 2 * SH * D], BF16, name="prod", align_bytes=64)
+            codes = prods.tile([P, 2 * SH * WORDS], U32, name="codes", align_bytes=64)
+            scales = prods.tile([P, 2 * SH * WORDS], U8, name="scales", align_bytes=64)
+            for sl in range(SH):
+                xt = transpose_unit(p_ld[r][:, sl * D:(sl + 1) * D])
+                nc.scalar.activation(
+                    out=grouped(prod[:, sl * D:(sl + 1) * D]), in_=bank_values(xt), func=FN.Square
+                )
+                nc.vector.tensor_tensor(
+                    out=grouped(prod[:, (SH + sl) * D:(SH + sl + 1) * D]),
+                    in0=bank_values(xt),
+                    in1=grouped(q_raw[:, bt * D:(bt + 1) * D]),
+                    op=ALU.mult,
+                )
+                if sl % 2 == 1:
+                    quantise(prod, codes, scales, sl - 1, 2)
+                    quantise(prod, codes, scales, SH + sl - 1, 2)
+            state[r] = (codes, scales)
+
+        def back(r):
+            bt, sh = divmod(r, S // SH)
+            codes, scales = state[r]
+            if sh == 0:
+                state["o"] = outs.tile([P, K * S], F32, name="o_sb")
+            o_sb = state["o"]
+            rn = epi.tile([P, K * SH], F32, name="rn")
+            dc = epi.tile([P, K * SH], F32, name="dc")
+            for kt in range(NKT):
+                npb = psn.tile([P, SH * P], F32, name="npb")
+                for sl in range(SH):
+                    mx_group(npb[:, sl * P:(sl + 1) * P], codes, scales, sl, kt)
+                dtb = psd.tile([P, SH * P], F32, name="dtb")
+                for sl in range(SH):
+                    mx_group(dtb[:, sl * P:(sl + 1) * P], codes, scales, SH + sl, kt)
+                cols = slice(kt * P * SH, (kt + 1) * P * SH)
+                nc.scalar.activation(
+                    out=rn[:, cols].rearrange("p (k s) -> p k s", s=SH),
+                    in_=npb[:].rearrange("p (s k) -> p k s", s=SH),
+                    func=FN.Abs_reciprocal_sqrt,
+                )
+                nc.vector.tensor_tensor(
+                    out=dc[:, cols].rearrange("p (k s) -> p k s", s=SH),
+                    in0=dtb[:].rearrange("p (s k) -> p k s", s=SH),
+                    in1=factor[:, bt * K + kt * P:bt * K + (kt + 1) * P].unsqueeze(2).to_broadcast([P, P, SH]),
+                    op=ALU.mult,
+                )
+                eng = nc.vector if kt in VECTOR_FINAL_KT else nc.gpsimd
+                o_cols = slice(kt * P * S, (kt + 1) * P * S)
+                eng.tensor_tensor(
+                    out=o_sb[:, o_cols].rearrange("p (k s) -> p k s", s=S)[:, :, sh * SH:(sh + 1) * SH],
+                    in0=dc[:, cols].rearrange("p (k s) -> p k s", s=SH),
+                    in1=rn[:, cols].rearrange("p (k s) -> p k s", s=SH),
+                    op=ALU.mult,
+                )
+                if sh == S // SH - 1:
+                    nc.sync.dma_start(out=out_flat[bt * P:(bt + 1) * P, o_cols], in_=o_sb[:, o_cols])
+
+        front(0)
+        for r in range(ROUNDS):
+            if r + 1 < ROUNDS:
+                front(r + 1)
+            back(r)

@@ -16,23 +16,29 @@ B, S, D, K = 512, 8, 1024, 512
 NBT = B // P
 NKT = K // P
 SH = 4
-ROUNDS = NBT * (S // SH)
+HALVES = S // SH
+ROUNDS = NBT * HALVES
 PASSES = D // 512
 WORDS = D // 4
 
 FLOPS = 2 * (2 * B * S + B) * K * D
 BYTES = 2 * (B * S * D + B * D + K * D) + 4 * B * S * K
 
-VECTOR_FINAL_KT = ()
+PINNED = True
+
+
+def final_on_vector(bt, kt):
+    return bt == NBT - 1 and kt >= 2
 
 
 def tile_mpl_t_kernel(tc, p, q, W, out):
     nc = tc.nc
     out_flat = out.rearrange("b s k -> b (s k)")
     with ExitStack() as ctx:
+        if PINNED:
+            ctx.enter_context(tc.manual_schedule())
         const = ctx.enter_context(tc.tile_pool(name="const", bufs=1))
-        loads = ctx.enter_context(tc.tile_pool(name="loads", bufs=8))
-        scratch = ctx.enter_context(tc.tile_pool(name="scratch", bufs=2))
+        loads = ctx.enter_context(tc.tile_pool(name="loads", bufs=6))
         prods = ctx.enter_context(tc.tile_pool(name="prods", bufs=2))
         epi = ctx.enter_context(tc.tile_pool(name="epi", bufs=2))
         outs = ctx.enter_context(tc.tile_pool(name="outs", bufs=2))
@@ -40,26 +46,61 @@ def tile_mpl_t_kernel(tc, p, q, W, out):
         psn = ctx.enter_context(tc.psum_pool(name="psn", bufs=2))
         psd = ctx.enter_context(tc.psum_pool(name="psd", bufs=2))
 
+        one = const.tile([P, 1], F32, name="one")
+        warm = const.tile([P, 1], F32, name="warm")
+        nc.vector.memset(one[:], 1.0)
+        nc.scalar.activation(out=warm[:], in_=one[:], func=FN.Abs_reciprocal_sqrt)
+
         ident = const.tile([P, P], F32, name="ident")
         make_identity(nc, ident[:])
 
-        w_ld = loads.tile([P, NKT * D], BF16, name="ld")
-        for kt in range(NKT):
-            nc.sync.dma_start(out=w_ld[:, kt * D:(kt + 1) * D], in_=W[kt * P:(kt + 1) * P, :])
-        q_ld = loads.tile([P, NBT * D], BF16, name="ld")
-        for bt in range(NBT):
-            nc.sync.dma_start(out=q_ld[:, bt * D:(bt + 1) * D], in_=q[bt * P:(bt + 1) * P, S - 1, :])
+        w_ld = const.tile([P, NKT * D], BF16, name="w_ld")
+        q_ld = const.tile([P, NBT * D], BF16, name="q_ld")
         p_ld = []
-        for r in range(ROUNDS):
-            bt, sh = divmod(r, S // SH)
+
+        def load_q(bt):
+            nc.sync.dma_start(out=q_ld[:, bt * D:(bt + 1) * D], in_=q[bt * P:(bt + 1) * P, S - 1, :])
+
+        def load_p(r, pieces):
+            bt, sh = divmod(r, HALVES)
             ld = loads.tile([P, SH * D], BF16, name="ld")
-            nc.sync.dma_start(
-                out=ld[:],
-                in_=p[bt * P:(bt + 1) * P, sh * SH:(sh + 1) * SH, :].rearrange("b s d -> b (s d)"),
-            )
+            n = SH // pieces
+            for i in range(pieces):
+                nc.sync.dma_start(
+                    out=ld[:, i * n * D:(i + 1) * n * D],
+                    in_=p[bt * P:(bt + 1) * P, sh * SH + i * n:sh * SH + (i + 1) * n, :].rearrange(
+                        "b s d -> b (s d)"
+                    ),
+                )
             p_ld.append(ld)
 
-        def transpose_unit(src):
+        for kt in range(NKT):
+            nc.sync.dma_start(out=w_ld[:, kt * D:(kt + 1) * D], in_=W[kt * P:(kt + 1) * P, :])
+        load_q(0)
+        load_p(0, SH)
+        load_p(1, 1)
+        for bt in range(1, NBT):
+            load_q(bt)
+        for r in range(2, ROUNDS):
+            load_p(r, 1)
+
+        w_sq = const.tile([P, NKT * D], BF16, name="w_sq", align_bytes=64)
+        w_codes = const.tile([P, NKT * WORDS], U32, name="w_codes", align_bytes=64)
+        w_scales = const.tile([P, NKT * WORDS], U8, name="w_scales", align_bytes=64)
+        w_raw = const.tile([P, D], BF16, name="w_raw")
+        q_raw = const.tile([P, NBT * D], BF16, name="q_raw")
+        q_sq = const.tile([P, NBT * D], BF16, name="q_sq", align_bytes=64)
+        q_codes = const.tile([P, NBT * WORDS], U32, name="q_codes", align_bytes=64)
+        q_scales = const.tile([P, NBT * WORDS], U8, name="q_scales", align_bytes=64)
+        factor = const.tile([P, NBT * K], F32, name="factor")
+
+        banks = {}
+        tiles = {}
+
+        def unit(ap, i):
+            return ap[:, i * D:(i + 1) * D]
+
+        def transposes(key, src):
             xt = psx.tile([P, 512], F32, name="xt")
             words = src.bitcast(F32)
             for g in range(PASSES):
@@ -69,16 +110,25 @@ def tile_mpl_t_kernel(tc, p, q, W, out):
                         in_=words[:, g * 256 + u * P:g * 256 + (u + 1) * P],
                         identity=ident[:],
                     )
-            return xt
+            banks[key] = xt
 
-        def bank_values(xt):
-            return xt[:].bitcast(BF16).rearrange("p (u c e) -> p c u e", u=2, e=2)
+        def t_p(r, sl):
+            transposes(("p", r, sl), unit(p_ld[r], sl))
 
-        def bank_words(xt):
-            return xt[:].rearrange("p (u c) -> p c u", u=2)
+        def bank_values(key):
+            return banks[key][:].bitcast(BF16).rearrange("p (u c e) -> p c u e", u=2, e=2)
 
         def grouped(ap):
             return ap.rearrange("p (c u e) -> p c u e", u=2, e=2)
+
+        def copy_words(key, dst):
+            nc.vector.tensor_copy(
+                out=dst.bitcast(F32).rearrange("p (c u) -> p c u", u=2),
+                in_=banks[key][:].rearrange("p (u c) -> p c u", u=2),
+            )
+
+        def square_bank(key, dst):
+            nc.scalar.activation(out=grouped(dst), in_=bank_values(key), func=FN.Square)
 
         def quantise(src, codes, scales, first, count):
             nc.vector.quantize_mx(
@@ -101,111 +151,206 @@ def tile_mpl_t_kernel(tc, p, q, W, out):
                     stop=(g == PASSES - 1),
                 )
 
-        w_sq = const.tile([P, NKT * D], BF16, name="w_sq", align_bytes=64)
-        w_codes = const.tile([P, NKT * WORDS], U32, name="w_codes", align_bytes=64)
-        w_scales = const.tile([P, NKT * WORDS], U8, name="w_scales", align_bytes=64)
-        for kt in range(NKT):
-            xt = transpose_unit(w_ld[:, kt * D:(kt + 1) * D])
-            dst = w_sq[:, kt * D:(kt + 1) * D]
-            if kt % 2 == 0:
-                nc.scalar.activation(out=grouped(dst), in_=bank_values(xt), func=FN.Square)
-            else:
-                raw = scratch.tile([P, D], BF16, name="raw")
-                nc.vector.tensor_copy(
-                    out=raw[:].bitcast(F32).rearrange("p (c u) -> p c u", u=2), in_=bank_words(xt)
-                )
-                nc.vector.tensor_tensor(out=dst, in0=raw[:], in1=raw[:], op=ALU.mult)
-            if kt % 2 == 1:
-                quantise(w_sq, w_codes, w_scales, kt - 1, 2)
+        def q_copy(bt):
+            copy_words(("q", bt), unit(q_raw, bt))
 
-        q_raw = const.tile([P, NBT * D], BF16, name="q_raw")
-        q_sq = const.tile([P, NBT * D], BF16, name="q_sq", align_bytes=64)
-        q_codes = const.tile([P, NBT * WORDS], U32, name="q_codes", align_bytes=64)
-        q_scales = const.tile([P, NBT * WORDS], U8, name="q_scales", align_bytes=64)
-        for bt in range(NBT):
-            xt = transpose_unit(q_ld[:, bt * D:(bt + 1) * D])
-            nc.vector.tensor_copy(
-                out=q_raw[:, bt * D:(bt + 1) * D].bitcast(F32).rearrange("p (c u) -> p c u", u=2),
-                in_=bank_words(xt),
-            )
-            nc.scalar.activation(
-                out=grouped(q_sq[:, bt * D:(bt + 1) * D]), in_=bank_values(xt), func=FN.Square
-            )
-            if bt % 2 == 1:
-                quantise(q_sq, q_codes, q_scales, bt - 1, 2)
+        def q_square(bt):
+            nc.gpsimd.tensor_tensor(out=unit(q_sq, bt), in0=unit(q_raw, bt), in1=unit(q_raw, bt), op=ALU.mult)
 
-        factor = const.tile([P, NBT * K], F32, name="factor")
-        for bt in range(NBT):
+        def q_quantise(bt):
+            quantise(q_sq, q_codes, q_scales, bt, 1)
+
+        def q_norms(bt):
             nq = psn.tile([P, K], F32, name="npb")
             for kt in range(NKT):
                 mx_group(nq[:, kt * P:(kt + 1) * P], q_codes, q_scales, bt, kt)
+            banks[("nq", bt)] = nq
+
+        def q_factor(bt):
             f = factor[:, bt * K:(bt + 1) * K]
-            nc.scalar.activation(out=f, in_=nq[:], func=FN.Abs_reciprocal_sqrt)
-            nc.vector.tensor_scalar_mul(out=f, in0=f, scalar1=-1.0 / D)
+            nc.scalar.activation(out=f, in_=banks[("nq", bt)][:], func=FN.Abs_reciprocal_sqrt)
+            nc.gpsimd.tensor_scalar(out=f, in0=f, scalar1=-1.0 / D, scalar2=0.0, op0=ALU.mult, op1=ALU.add)
 
-        state = {}
+        def round_tile(r, name, shape, dtype):
+            if (name, r) not in tiles:
+                tiles[(name, r)] = prods.tile(shape, dtype, name=name, align_bytes=64)
+            return tiles[(name, r)]
 
-        def front(r):
-            bt = r // (S // SH)
-            prod = prods.tile([P, 2 * SH * D], BF16, name="prod", align_bytes=64)
-            codes = prods.tile([P, 2 * SH * WORDS], U32, name="codes", align_bytes=64)
-            scales = prods.tile([P, 2 * SH * WORDS], U8, name="scales", align_bytes=64)
+        def prod_of(r):
+            return round_tile(r, "prod", [P, 2 * SH * D], BF16)
+
+        def sq(r, sl):
+            square_bank(("p", r, sl), unit(prod_of(r), sl))
+
+        def pq(r, sl):
+            nc.vector.tensor_tensor(
+                out=grouped(unit(prod_of(r), SH + sl)),
+                in0=bank_values(("p", r, sl)),
+                in1=grouped(unit(q_raw, r // HALVES)),
+                op=ALU.mult,
+            )
+
+        def quant(r, first, count):
+            quantise(
+                prod_of(r),
+                round_tile(r, "codes", [P, 2 * SH * WORDS], U32),
+                round_tile(r, "scales", [P, 2 * SH * WORDS], U8),
+                first,
+                count,
+            )
+
+        def mx(r, kt):
+            codes = tiles[("codes", r)]
+            scales = tiles[("scales", r)]
+            dtb = psd.tile([P, SH * P], F32, name="dtb")
             for sl in range(SH):
-                xt = transpose_unit(p_ld[r][:, sl * D:(sl + 1) * D])
-                nc.scalar.activation(
-                    out=grouped(prod[:, sl * D:(sl + 1) * D]), in_=bank_values(xt), func=FN.Square
-                )
-                nc.vector.tensor_tensor(
-                    out=grouped(prod[:, (SH + sl) * D:(SH + sl + 1) * D]),
-                    in0=bank_values(xt),
-                    in1=grouped(q_raw[:, bt * D:(bt + 1) * D]),
-                    op=ALU.mult,
-                )
-                if sl % 2 == 1:
-                    quantise(prod, codes, scales, sl - 1, 2)
-                    quantise(prod, codes, scales, SH + sl - 1, 2)
-            state[r] = (codes, scales)
+                mx_group(dtb[:, sl * P:(sl + 1) * P], codes, scales, SH + sl, kt)
+            npb = psn.tile([P, SH * P], F32, name="npb")
+            for sl in range(SH):
+                mx_group(npb[:, sl * P:(sl + 1) * P], codes, scales, sl, kt)
+            banks[("dot", r, kt)] = dtb
+            banks[("np", r, kt)] = npb
 
-        def back(r):
-            bt, sh = divmod(r, S // SH)
-            codes, scales = state[r]
-            if sh == 0:
-                state["o"] = outs.tile([P, K * S], F32, name="o_sb")
-            o_sb = state["o"]
-            rn = epi.tile([P, K * SH], F32, name="rn")
-            dc = epi.tile([P, K * SH], F32, name="dc")
-            for kt in range(NKT):
-                npb = psn.tile([P, SH * P], F32, name="npb")
-                for sl in range(SH):
-                    mx_group(npb[:, sl * P:(sl + 1) * P], codes, scales, sl, kt)
-                dtb = psd.tile([P, SH * P], F32, name="dtb")
-                for sl in range(SH):
-                    mx_group(dtb[:, sl * P:(sl + 1) * P], codes, scales, SH + sl, kt)
-                cols = slice(kt * P * SH, (kt + 1) * P * SH)
-                nc.scalar.activation(
-                    out=rn[:, cols].rearrange("p (k s) -> p k s", s=SH),
-                    in_=npb[:].rearrange("p (s k) -> p k s", s=SH),
-                    func=FN.Abs_reciprocal_sqrt,
-                )
-                nc.vector.tensor_tensor(
-                    out=dc[:, cols].rearrange("p (k s) -> p k s", s=SH),
-                    in0=dtb[:].rearrange("p (s k) -> p k s", s=SH),
-                    in1=factor[:, bt * K + kt * P:bt * K + (kt + 1) * P].unsqueeze(2).to_broadcast([P, P, SH]),
-                    op=ALU.mult,
-                )
-                eng = nc.vector if kt in VECTOR_FINAL_KT else nc.gpsimd
-                o_cols = slice(kt * P * S, (kt + 1) * P * S)
-                eng.tensor_tensor(
-                    out=o_sb[:, o_cols].rearrange("p (k s) -> p k s", s=S)[:, :, sh * SH:(sh + 1) * SH],
-                    in0=dc[:, cols].rearrange("p (k s) -> p k s", s=SH),
-                    in1=rn[:, cols].rearrange("p (k s) -> p k s", s=SH),
-                    op=ALU.mult,
-                )
-                if sh == S // SH - 1:
-                    nc.sync.dma_start(out=out_flat[bt * P:(bt + 1) * P, o_cols], in_=o_sb[:, o_cols])
+        def epi_tile(r, name):
+            if (name, r) not in tiles:
+                tiles[(name, r)] = epi.tile([P, K * SH], F32, name=name)
+            return tiles[(name, r)]
 
-        front(0)
+        def ks(ap, s):
+            return ap.rearrange("p (k s) -> p k s", s=s)
+
+        def chunk(ap, kt):
+            return ks(ap[:, kt * P * SH:(kt + 1) * P * SH], SH)
+
+        def rs(r, kt):
+            nc.scalar.activation(
+                out=chunk(epi_tile(r, "rn"), kt),
+                in_=banks[("np", r, kt)][:].rearrange("p (s k) -> p k s", s=SH),
+                func=FN.Abs_reciprocal_sqrt,
+            )
+
+        def dc(r, kt):
+            bt = r // HALVES
+            nc.vector.tensor_tensor(
+                out=chunk(epi_tile(r, "dc"), kt),
+                in0=banks[("dot", r, kt)][:].rearrange("p (s k) -> p k s", s=SH),
+                in1=factor[:, bt * K + kt * P:bt * K + (kt + 1) * P].unsqueeze(2).to_broadcast([P, P, SH]),
+                op=ALU.mult,
+            )
+
+        def fin(r, kt):
+            bt, sh = divmod(r, HALVES)
+            if ("o", bt) not in tiles:
+                tiles[("o", bt)] = outs.tile([P, K * S], F32, name="o_sb")
+            o_sb = tiles[("o", bt)]
+            o_cols = slice(kt * P * S, (kt + 1) * P * S)
+            eng = nc.vector if final_on_vector(bt, kt) else nc.gpsimd
+            eng.tensor_tensor(
+                out=ks(o_sb[:, o_cols], S)[:, :, sh * SH:(sh + 1) * SH],
+                in0=chunk(tiles[("dc", r)], kt),
+                in1=chunk(tiles[("rn", r)], kt),
+                op=ALU.mult,
+            )
+            if sh == HALVES - 1:
+                nc.sync.dma_start(out=out_flat[bt * P:(bt + 1) * P, o_cols], in_=o_sb[:, o_cols])
+
+        for kt in range(NKT):
+            transposes(("w", kt), unit(w_ld, kt))
+        square_bank(("w", 0), unit(w_sq, 0))
+        copy_words(("w", 1), w_raw[:])
+        nc.vector.tensor_tensor(out=unit(w_sq, 1), in0=w_raw[:], in1=w_raw[:], op=ALU.mult)
+        square_bank(("w", 2), unit(w_sq, 2))
+        square_bank(("w", 3), unit(w_sq, 3))
+        quantise(w_sq, w_codes, w_scales, 0, 2)
+        transposes(("q", 0), unit(q_ld, 0))
+        t_p(0, 0)
+        t_p(0, 1)
+        t_p(0, 2)
+        q_copy(0)
+        q_square(0)
+        quantise(w_sq, w_codes, w_scales, 2, 2)
+        sq(0, 0)
+        pq(0, 0)
+        t_p(0, 3)
+        sq(0, 1)
+        pq(0, 1)
+        t_p(1, 0)
+        q_quantise(0)
+        sq(0, 2)
+        pq(0, 2)
+        quant(0, 4, 2)
+        t_p(1, 1)
+        q_norms(0)
+        sq(0, 3)
+        quant(0, 0, 2)
+        pq(0, 3)
+        quant(0, 6, 2)
+        quant(0, 2, 1)
+        t_p(1, 2)
+        t_p(1, 3)
+        q_factor(0)
+
+        def period(r):
+            nxt = r + 1 < ROUNDS
+            bt_next = r // HALVES + 1
+            early_q = r % HALVES == 0 and bt_next < NBT
+            late_q = r % HALVES == 1 and bt_next < NBT
+            late_fin = final_on_vector(r // HALVES, 2)
+            if nxt:
+                pq(r + 1, 0)
+            quant(r, 3, 1)
+            if r > 0:
+                rs(r - 1, 3)
+                fin(r - 1, 3)
+            if nxt:
+                sq(r + 1, 0)
+                pq(r + 1, 1)
+                pq(r + 1, 2)
+            mx(r, 0)
+            dc(r, 0)
+            rs(r, 0)
+            fin(r, 0)
+            if nxt:
+                pq(r + 1, 3)
+                sq(r + 1, 1)
+                quant(r + 1, 4, 2)
+            if late_q:
+                q_quantise(bt_next)
+            mx(r, 1)
+            dc(r, 1)
+            rs(r, 1)
+            fin(r, 1)
+            if early_q:
+                transposes(("q", bt_next), unit(q_ld, bt_next))
+            if late_q:
+                q_norms(bt_next)
+            if nxt:
+                sq(r + 1, 2)
+                quant(r + 1, 6, 2)
+            if early_q:
+                q_copy(bt_next)
+                q_square(bt_next)
+            if late_q:
+                q_factor(bt_next)
+            mx(r, 2)
+            dc(r, 2)
+            rs(r, 2)
+            if not late_fin:
+                fin(r, 2)
+            if nxt:
+                quant(r + 1, 0, 2)
+                sq(r + 1, 3)
+            mx(r, 3)
+            dc(r, 3)
+            if late_fin:
+                fin(r, 2)
+            if nxt:
+                quant(r + 1, 2, 1)
+            if r + 2 < ROUNDS:
+                for sl in range(SH):
+                    t_p(r + 2, sl)
+
         for r in range(ROUNDS):
-            if r + 1 < ROUNDS:
-                front(r + 1)
-            back(r)
+            period(r)
+        rs(ROUNDS - 1, 3)
+        fin(ROUNDS - 1, 3)

@@ -25,10 +25,8 @@ FLOPS = 2 * (2 * B * S + B) * K * D
 BYTES = 2 * (B * S * D + B * D + K * D) + 4 * B * S * K
 
 PINNED = True
-
-
-def final_on_vector(bt, kt):
-    return bt == NBT - 1 and kt >= 2
+HALF_K = K // 2
+VECTOR_K = 64
 
 
 def tile_mpl_t_kernel(tc, p, q, W, out):
@@ -87,7 +85,7 @@ def tile_mpl_t_kernel(tc, p, q, W, out):
         w_sq = const.tile([P, NKT * D], BF16, name="w_sq", align_bytes=64)
         w_codes = const.tile([P, NKT * WORDS], U32, name="w_codes", align_bytes=64)
         w_scales = const.tile([P, NKT * WORDS], U8, name="w_scales", align_bytes=64)
-        w_raw = const.tile([P, D], BF16, name="w_raw")
+        w_raw = const.tile([P, 2 * D], BF16, name="w_raw")
         q_raw = const.tile([P, NBT * D], BF16, name="q_raw")
         q_sq = const.tile([P, NBT * D], BF16, name="q_sq", align_bytes=64)
         q_codes = const.tile([P, NBT * WORDS], U32, name="q_codes", align_bytes=64)
@@ -121,8 +119,9 @@ def tile_mpl_t_kernel(tc, p, q, W, out):
         def grouped(ap):
             return ap.rearrange("p (c u e) -> p c u e", u=2, e=2)
 
-        def copy_words(key, dst):
-            nc.vector.tensor_copy(
+        def copy_words(key, dst, on_scalar):
+            copy = nc.scalar.copy if on_scalar else nc.vector.tensor_copy
+            copy(
                 out=dst.bitcast(F32).rearrange("p (c u) -> p c u", u=2),
                 in_=banks[key][:].rearrange("p (u c) -> p c u", u=2),
             )
@@ -152,10 +151,10 @@ def tile_mpl_t_kernel(tc, p, q, W, out):
                 )
 
         def q_copy(bt):
-            copy_words(("q", bt), unit(q_raw, bt))
+            copy_words(("q", bt), unit(q_raw, bt), bt > 0)
 
         def q_square(bt):
-            nc.gpsimd.tensor_tensor(out=unit(q_sq, bt), in0=unit(q_raw, bt), in1=unit(q_raw, bt), op=ALU.mult)
+            nc.vector.tensor_tensor(out=unit(q_sq, bt), in0=unit(q_raw, bt), in1=unit(q_raw, bt), op=ALU.mult)
 
         def q_quantise(bt):
             quantise(q_sq, q_codes, q_scales, bt, 1)
@@ -169,7 +168,6 @@ def tile_mpl_t_kernel(tc, p, q, W, out):
         def q_factor(bt):
             f = factor[:, bt * K:(bt + 1) * K]
             nc.scalar.activation(out=f, in_=banks[("nq", bt)][:], func=FN.Abs_reciprocal_sqrt)
-            nc.gpsimd.tensor_scalar(out=f, in0=f, scalar1=-1.0 / D, scalar2=0.0, op0=ALU.mult, op1=ALU.add)
 
         def round_tile(r, name, shape, dtype):
             if (name, r) not in tiles:
@@ -179,24 +177,30 @@ def tile_mpl_t_kernel(tc, p, q, W, out):
         def prod_of(r):
             return round_tile(r, "prod", [P, 2 * SH * D], BF16)
 
+        def pp_unit(sl):
+            return (sl // 2) * 4 + sl % 2
+
+        def pq_unit(sl):
+            return (sl // 2) * 4 + 2 + sl % 2
+
         def sq(r, sl):
-            square_bank(("p", r, sl), unit(prod_of(r), sl))
+            square_bank(("p", r, sl), unit(prod_of(r), pp_unit(sl)))
 
         def pq(r, sl):
             nc.vector.tensor_tensor(
-                out=grouped(unit(prod_of(r), SH + sl)),
+                out=grouped(unit(prod_of(r), pq_unit(sl))),
                 in0=bank_values(("p", r, sl)),
                 in1=grouped(unit(q_raw, r // HALVES)),
                 op=ALU.mult,
             )
 
-        def quant(r, first, count):
+        def quant(r, half):
             quantise(
                 prod_of(r),
                 round_tile(r, "codes", [P, 2 * SH * WORDS], U32),
                 round_tile(r, "scales", [P, 2 * SH * WORDS], U8),
-                first,
-                count,
+                4 * half,
+                4,
             )
 
         def mx(r, kt):
@@ -204,10 +208,10 @@ def tile_mpl_t_kernel(tc, p, q, W, out):
             scales = tiles[("scales", r)]
             dtb = psd.tile([P, SH * P], F32, name="dtb")
             for sl in range(SH):
-                mx_group(dtb[:, sl * P:(sl + 1) * P], codes, scales, SH + sl, kt)
+                mx_group(dtb[:, sl * P:(sl + 1) * P], codes, scales, pq_unit(sl), kt)
             npb = psn.tile([P, SH * P], F32, name="npb")
             for sl in range(SH):
-                mx_group(npb[:, sl * P:(sl + 1) * P], codes, scales, sl, kt)
+                mx_group(npb[:, sl * P:(sl + 1) * P], codes, scales, pp_unit(sl), kt)
             banks[("dot", r, kt)] = dtb
             banks[("np", r, kt)] = npb
 
@@ -231,126 +235,121 @@ def tile_mpl_t_kernel(tc, p, q, W, out):
 
         def dc(r, kt):
             bt = r // HALVES
-            nc.vector.tensor_tensor(
+            nc.vector.scalar_tensor_tensor(
                 out=chunk(epi_tile(r, "dc"), kt),
                 in0=banks[("dot", r, kt)][:].rearrange("p (s k) -> p k s", s=SH),
+                scalar=-1.0 / D,
                 in1=factor[:, bt * K + kt * P:bt * K + (kt + 1) * P].unsqueeze(2).to_broadcast([P, P, SH]),
-                op=ALU.mult,
+                op0=ALU.mult,
+                op1=ALU.mult,
             )
 
-        def fin(r, kt):
+        def fin_part(eng, r, k0, k1):
             bt, sh = divmod(r, HALVES)
             if ("o", bt) not in tiles:
                 tiles[("o", bt)] = outs.tile([P, K * S], F32, name="o_sb")
-            o_sb = tiles[("o", bt)]
-            o_cols = slice(kt * P * S, (kt + 1) * P * S)
-            eng = nc.vector if final_on_vector(bt, kt) else nc.gpsimd
             eng.tensor_tensor(
-                out=ks(o_sb[:, o_cols], S)[:, :, sh * SH:(sh + 1) * SH],
-                in0=chunk(tiles[("dc", r)], kt),
-                in1=chunk(tiles[("rn", r)], kt),
+                out=ks(tiles[("o", bt)][:, k0 * S:k1 * S], S)[:, :, sh * SH:(sh + 1) * SH],
+                in0=ks(tiles[("dc", r)][:, k0 * SH:k1 * SH], SH),
+                in1=ks(tiles[("rn", r)][:, k0 * SH:k1 * SH], SH),
                 op=ALU.mult,
             )
+
+        def fin(r, h):
+            bt, sh = divmod(r, HALVES)
+            fin_part(nc.vector, r, h * HALF_K, h * HALF_K + VECTOR_K)
+            fin_part(nc.gpsimd, r, h * HALF_K + VECTOR_K, (h + 1) * HALF_K)
             if sh == HALVES - 1:
-                nc.sync.dma_start(out=out_flat[bt * P:(bt + 1) * P, o_cols], in_=o_sb[:, o_cols])
+                cols = slice(h * HALF_K * S, (h + 1) * HALF_K * S)
+                nc.sync.dma_start(out=out_flat[bt * P:(bt + 1) * P, cols], in_=tiles[("o", bt)][:, cols])
 
         for kt in range(NKT):
             transposes(("w", kt), unit(w_ld, kt))
-        square_bank(("w", 0), unit(w_sq, 0))
-        copy_words(("w", 1), w_raw[:])
-        nc.vector.tensor_tensor(out=unit(w_sq, 1), in0=w_raw[:], in1=w_raw[:], op=ALU.mult)
-        square_bank(("w", 2), unit(w_sq, 2))
-        square_bank(("w", 3), unit(w_sq, 3))
-        quantise(w_sq, w_codes, w_scales, 0, 2)
+        for kt in range(NKT):
+            if kt % 2 == 0:
+                copy_words(("w", kt), unit(w_raw, kt // 2), False)
+                nc.vector.tensor_tensor(
+                    out=unit(w_sq, kt), in0=unit(w_raw, kt // 2), in1=unit(w_raw, kt // 2), op=ALU.mult
+                )
+            else:
+                square_bank(("w", kt), unit(w_sq, kt))
         transposes(("q", 0), unit(q_ld, 0))
         t_p(0, 0)
         t_p(0, 1)
         t_p(0, 2)
         q_copy(0)
         q_square(0)
+        quantise(w_sq, w_codes, w_scales, 0, 2)
         quantise(w_sq, w_codes, w_scales, 2, 2)
-        sq(0, 0)
-        pq(0, 0)
+        q_quantise(0)
         t_p(0, 3)
+        sq(0, 0)
         sq(0, 1)
+        pq(0, 0)
         pq(0, 1)
         t_p(1, 0)
-        q_quantise(0)
-        sq(0, 2)
-        pq(0, 2)
-        quant(0, 4, 2)
         t_p(1, 1)
         q_norms(0)
+        sq(0, 2)
+        quant(0, 0)
         sq(0, 3)
-        quant(0, 0, 2)
+        pq(0, 2)
         pq(0, 3)
-        quant(0, 6, 2)
-        quant(0, 2, 1)
         t_p(1, 2)
         t_p(1, 3)
-        q_factor(0)
 
         def period(r):
             nxt = r + 1 < ROUNDS
-            bt_next = r // HALVES + 1
-            early_q = r % HALVES == 0 and bt_next < NBT
-            late_q = r % HALVES == 1 and bt_next < NBT
-            late_fin = final_on_vector(r // HALVES, 2)
-            if nxt:
-                pq(r + 1, 0)
-            quant(r, 3, 1)
-            if r > 0:
-                rs(r - 1, 3)
-                fin(r - 1, 3)
+            bt = r // HALVES
+            early_q = r % HALVES == 0 and bt + 1 < NBT
+            late_q = r % HALVES == 1 and bt + 1 < NBT
             if nxt:
                 sq(r + 1, 0)
-                pq(r + 1, 1)
-                pq(r + 1, 2)
-            mx(r, 0)
-            dc(r, 0)
-            rs(r, 0)
-            fin(r, 0)
-            if nxt:
-                pq(r + 1, 3)
                 sq(r + 1, 1)
-                quant(r + 1, 4, 2)
-            if late_q:
-                q_quantise(bt_next)
-            mx(r, 1)
-            dc(r, 1)
-            rs(r, 1)
-            fin(r, 1)
-            if early_q:
-                transposes(("q", bt_next), unit(q_ld, bt_next))
-            if late_q:
-                q_norms(bt_next)
+            if r == 0:
+                q_factor(0)
             if nxt:
                 sq(r + 1, 2)
-                quant(r + 1, 6, 2)
-            if early_q:
-                q_copy(bt_next)
-                q_square(bt_next)
+            quant(r, 1)
             if late_q:
-                q_factor(bt_next)
-            mx(r, 2)
-            dc(r, 2)
-            rs(r, 2)
-            if not late_fin:
-                fin(r, 2)
+                q_square(bt + 1)
+            if r > 0:
+                fin(r - 1, 1)
             if nxt:
-                quant(r + 1, 0, 2)
+                pq(r + 1, 0)
+                pq(r + 1, 1)
+            mx(r, 0)
+            mx(r, 1)
+            dc(r, 0)
+            dc(r, 1)
+            rs(r, 0)
+            if nxt:
                 sq(r + 1, 3)
-            mx(r, 3)
-            dc(r, 3)
-            if late_fin:
-                fin(r, 2)
+            rs(r, 1)
+            if early_q:
+                transposes(("q", bt + 1), unit(q_ld, bt + 1))
+                q_copy(bt + 1)
             if nxt:
-                quant(r + 1, 2, 1)
+                quant(r + 1, 0)
+            if late_q:
+                q_quantise(bt + 1)
+            fin(r, 0)
+            if nxt:
+                pq(r + 1, 2)
+                pq(r + 1, 3)
+            mx(r, 2)
+            mx(r, 3)
+            dc(r, 2)
+            dc(r, 3)
+            rs(r, 2)
+            rs(r, 3)
+            if late_q:
+                q_norms(bt + 1)
+                q_factor(bt + 1)
             if r + 2 < ROUNDS:
                 for sl in range(SH):
                     t_p(r + 2, sl)
 
         for r in range(ROUNDS):
             period(r)
-        rs(ROUNDS - 1, 3)
-        fin(ROUNDS - 1, 3)
+        fin(ROUNDS - 1, 1)

@@ -257,11 +257,21 @@ def tile_mpl_t_kernel(tc, p, q, W, out):
 
         def fin(r, h):
             bt, sh = divmod(r, HALVES)
+            if bt == NBT - 1:
+                return
             fin_part(nc.vector, r, h * HALF_K, h * HALF_K + VECTOR_K)
             fin_part(nc.gpsimd, r, h * HALF_K + VECTOR_K, (h + 1) * HALF_K)
             if sh == HALVES - 1:
                 cols = slice(h * HALF_K * S, (h + 1) * HALF_K * S)
                 nc.sync.dma_start(out=out_flat[bt * P:(bt + 1) * P, cols], in_=tiles[("o", bt)][:, cols])
+
+        def fin_last(r, kt):
+            fin_part(nc.vector, r, kt * P, (kt + 1) * P)
+            if r == ROUNDS - 1:
+                cols = slice(kt * P * S, (kt + 1) * P * S)
+                nc.sync.dma_start(
+                    out=out_flat[(NBT - 1) * P:NBT * P, cols], in_=tiles[("o", NBT - 1)][:, cols]
+                )
 
         for kt in range(NKT):
             transposes(("w", kt), unit(w_ld, kt))
@@ -318,9 +328,13 @@ def tile_mpl_t_kernel(tc, p, q, W, out):
             if nxt:
                 pq(r + 1, 0)
                 pq(r + 1, 1)
+            else:
+                fin_last(r - 1, 0)
             mx(r, 0)
             mx(r, 1)
             dc(r, 0)
+            if not nxt:
+                fin_last(r - 1, 1)
             dc(r, 1)
             rs(r, 0)
             if nxt:
@@ -337,12 +351,21 @@ def tile_mpl_t_kernel(tc, p, q, W, out):
             if nxt:
                 pq(r + 1, 2)
                 pq(r + 1, 3)
+            else:
+                fin_last(r - 1, 2)
+                fin_last(r, 0)
             mx(r, 2)
             mx(r, 3)
             dc(r, 2)
+            if not nxt:
+                fin_last(r - 1, 3)
+                fin_last(r, 1)
             dc(r, 3)
             rs(r, 2)
             rs(r, 3)
+            if not nxt:
+                fin_last(r, 2)
+                fin_last(r, 3)
             if late_q:
                 q_norms(bt + 1)
                 q_factor(bt + 1)
@@ -352,4 +375,3 @@ def tile_mpl_t_kernel(tc, p, q, W, out):
 
         for r in range(ROUNDS):
             period(r)
-        fin(ROUNDS - 1, 1)

@@ -24,7 +24,7 @@ WORDS = D // 4
 FLOPS = 2 * (2 * B * S + B) * K * D
 BYTES = 2 * (B * S * D + B * D + K * D) + 4 * B * S * K
 
-PINNED = True
+PINNED = False
 HALF_K = K // 2
 VECTOR_K = 64
 

from contextlib import ExitStack

import concourse.mybir as mybir
from concourse.masks import make_identity

F32 = mybir.dt.float32
BF16 = mybir.dt.bfloat16
U32 = mybir.dt.uint32
U8 = mybir.dt.uint8
FP8X4 = mybir.dt.float8_e4m3fn_x4
FN = mybir.ActivationFunctionType
ALU = mybir.AluOpType

P = 128
B, S, D, K = 512, 8, 1024, 512
NBT = B // P
NKT = K // P
SH = 4
HALVES = S // SH
ROUNDS = NBT * HALVES
PASSES = D // 512
WORDS = D // 4

FLOPS = 2 * (2 * B * S + B) * K * D
BYTES = 2 * (B * S * D + B * D + K * D) + 4 * B * S * K

PINNED = False
HALF_K = K // 2
VECTOR_K = 64


def tile_mpl_t_kernel(tc, p, q, W, out):
    nc = tc.nc
    out_flat = out.rearrange("b s k -> b (s k)")
    with ExitStack() as ctx:
        if PINNED:
            ctx.enter_context(tc.manual_schedule())
        const = ctx.enter_context(tc.tile_pool(name="const", bufs=1))
        loads = ctx.enter_context(tc.tile_pool(name="loads", bufs=6))
        prods = ctx.enter_context(tc.tile_pool(name="prods", bufs=2))
        epi = ctx.enter_context(tc.tile_pool(name="epi", bufs=2))
        outs = ctx.enter_context(tc.tile_pool(name="outs", bufs=2))
        psx = ctx.enter_context(tc.psum_pool(name="psx", bufs=4))
        psn = ctx.enter_context(tc.psum_pool(name="psn", bufs=2))
        psd = ctx.enter_context(tc.psum_pool(name="psd", bufs=2))

        one = const.tile([P, 1], F32, name="one")
        warm = const.tile([P, 1], F32, name="warm")
        nc.vector.memset(one[:], 1.0)
        nc.scalar.activation(out=warm[:], in_=one[:], func=FN.Abs_reciprocal_sqrt)

        ident = const.tile([P, P], F32, name="ident")
        make_identity(nc, ident[:])

        w_ld = const.tile([P, NKT * D], BF16, name="w_ld")
        q_ld = const.tile([P, NBT * D], BF16, name="q_ld")
        p_ld = []

        def load_q(bt):
            nc.sync.dma_start(out=q_ld[:, bt * D:(bt + 1) * D], in_=q[bt * P:(bt + 1) * P, S - 1, :])

        def load_p(r, pieces):
            bt, sh = divmod(r, HALVES)
            ld = loads.tile([P, SH * D], BF16, name="ld")
            n = SH // pieces
            for i in range(pieces):
                nc.sync.dma_start(
                    out=ld[:, i * n * D:(i + 1) * n * D],
                    in_=p[bt * P:(bt + 1) * P, sh * SH + i * n:sh * SH + (i + 1) * n, :].rearrange(
                        "b s d -> b (s d)"
                    ),
                )
            p_ld.append(ld)

        for kt in range(NKT):
            nc.sync.dma_start(out=w_ld[:, kt * D:(kt + 1) * D], in_=W[kt * P:(kt + 1) * P, :])
        load_q(0)
        load_p(0, SH)
        load_p(1, 1)
        for bt in range(1, NBT):
            load_q(bt)
        for r in range(2, ROUNDS):
            load_p(r, 1)

        w_sq = const.tile([P, NKT * D], BF16, name="w_sq", align_bytes=64)
        w_codes = const.tile([P, NKT * WORDS], U32, name="w_codes", align_bytes=64)
        w_scales = const.tile([P, NKT * WORDS], U8, name="w_scales", align_bytes=64)
        w_raw = const.tile([P, 2 * D], BF16, name="w_raw")
        q_raw = const.tile([P, NBT * D], BF16, name="q_raw")
        q_sq = const.tile([P, NBT * D], BF16, name="q_sq", align_bytes=64)
        q_codes = const.tile([P, NBT * WORDS], U32, name="q_codes", align_bytes=64)
        q_scales = const.tile([P, NBT * WORDS], U8, name="q_scales", align_bytes=64)
        factor = const.tile([P, NBT * K], F32, name="factor")

        banks = {}
        tiles = {}

        def unit(ap, i):
            return ap[:, i * D:(i + 1) * D]

        def transposes(key, src):
            xt = psx.tile([P, 512], F32, name="xt")
            words = src.bitcast(F32)
            for g in range(PASSES):
                for u in range(2):
                    nc.tensor.transpose(
                        out=xt[:, u * 256 + g * P:u * 256 + (g + 1) * P],
                        in_=words[:, g * 256 + u * P:g * 256 + (u + 1) * P],
                        identity=ident[:],
                    )
            banks[key] = xt

        def t_p(r, sl):
            transposes(("p", r, sl), unit(p_ld[r], sl))

        def bank_values(key):
            return banks[key][:].bitcast(BF16).rearrange("p (u c e) -> p c u e", u=2, e=2)

        def grouped(ap):
            return ap.rearrange("p (c u e) -> p c u e", u=2, e=2)

        def copy_words(key, dst, on_scalar):
            copy = nc.scalar.copy if on_scalar else nc.vector.tensor_copy
            copy(
                out=dst.bitcast(F32).rearrange("p (c u) -> p c u", u=2),
                in_=banks[key][:].rearrange("p (u c) -> p c u", u=2),
            )

        def square_bank(key, dst):
            nc.scalar.activation(out=grouped(dst), in_=bank_values(key), func=FN.Square)

        def quantise(src, codes, scales, first, count):
            nc.vector.quantize_mx(
                out=codes[:, first * WORDS:(first + count) * WORDS].bitcast(FP8X4),
                scales=scales[:, first * WORDS:(first + count) * WORDS],
                in_=src[:, first * D:(first + count) * D],
            )

        def mx_group(dst, a_codes, a_scales, a_unit, kt):
            for g in range(PASSES):
                a0 = a_unit * WORDS + g * P
                w0 = kt * WORDS + g * P
                nc.tensor.matmul_mx(
                    out=dst,
                    lhsT=a_codes[:, a0:a0 + P].bitcast(FP8X4),
                    lhsT_scale=a_scales[:, a0:a0 + P],
                    rhs=w_codes[:, w0:w0 + P].bitcast(FP8X4),
                    rhs_scale=w_scales[:, w0:w0 + P],
                    start=(g == 0),
                    stop=(g == PASSES - 1),
                )

        def q_copy(bt):
            copy_words(("q", bt), unit(q_raw, bt), bt > 0)

        def q_square(bt):
            nc.vector.tensor_tensor(out=unit(q_sq, bt), in0=unit(q_raw, bt), in1=unit(q_raw, bt), op=ALU.mult)

        def q_quantise(bt):
            quantise(q_sq, q_codes, q_scales, bt, 1)

        def q_norms(bt):
            nq = psn.tile([P, K], F32, name="npb")
            for kt in range(NKT):
                mx_group(nq[:, kt * P:(kt + 1) * P], q_codes, q_scales, bt, kt)
            banks[("nq", bt)] = nq

        def q_factor(bt):
            f = factor[:, bt * K:(bt + 1) * K]
            nc.scalar.activation(out=f, in_=banks[("nq", bt)][:], func=FN.Abs_reciprocal_sqrt)

        def round_tile(r, name, shape, dtype):
            if (name, r) not in tiles:
                tiles[(name, r)] = prods.tile(shape, dtype, name=name, align_bytes=64)
            return tiles[(name, r)]

        def prod_of(r):
            return round_tile(r, "prod", [P, 2 * SH * D], BF16)

        def pp_unit(sl):
            return (sl // 2) * 4 + sl % 2

        def pq_unit(sl):
            return (sl // 2) * 4 + 2 + sl % 2

        def sq(r, sl):
            square_bank(("p", r, sl), unit(prod_of(r), pp_unit(sl)))

        def pq(r, sl):
            nc.vector.tensor_tensor(
                out=grouped(unit(prod_of(r), pq_unit(sl))),
                in0=bank_values(("p", r, sl)),
                in1=grouped(unit(q_raw, r // HALVES)),
                op=ALU.mult,
            )

        def quant(r, half):
            quantise(
                prod_of(r),
                round_tile(r, "codes", [P, 2 * SH * WORDS], U32),
                round_tile(r, "scales", [P, 2 * SH * WORDS], U8),
                4 * half,
                4,
            )

        def mx(r, kt):
            codes = tiles[("codes", r)]
            scales = tiles[("scales", r)]
            dtb = psd.tile([P, SH * P], F32, name="dtb")
            for sl in range(SH):
                mx_group(dtb[:, sl * P:(sl + 1) * P], codes, scales, pq_unit(sl), kt)
            npb = psn.tile([P, SH * P], F32, name="npb")
            for sl in range(SH):
                mx_group(npb[:, sl * P:(sl + 1) * P], codes, scales, pp_unit(sl), kt)
            banks[("dot", r, kt)] = dtb
            banks[("np", r, kt)] = npb

        def epi_tile(r, name):
            if (name, r) not in tiles:
                tiles[(name, r)] = epi.tile([P, K * SH], F32, name=name)
            return tiles[(name, r)]

        def ks(ap, s):
            return ap.rearrange("p (k s) -> p k s", s=s)

        def chunk(ap, kt):
            return ks(ap[:, kt * P * SH:(kt + 1) * P * SH], SH)

        def rs(r, kt):
            nc.scalar.activation(
                out=chunk(epi_tile(r, "rn"), kt),
                in_=banks[("np", r, kt)][:].rearrange("p (s k) -> p k s", s=SH),
                func=FN.Abs_reciprocal_sqrt,
            )

        def dc(r, kt):
            bt = r // HALVES
            nc.vector.scalar_tensor_tensor(
                out=chunk(epi_tile(r, "dc"), kt),
                in0=banks[("dot", r, kt)][:].rearrange("p (s k) -> p k s", s=SH),
                scalar=-1.0 / D,
                in1=factor[:, bt * K + kt * P:bt * K + (kt + 1) * P].unsqueeze(2).to_broadcast([P, P, SH]),
                op0=ALU.mult,
                op1=ALU.mult,
            )

        def fin_part(eng, r, k0, k1):
            bt, sh = divmod(r, HALVES)
            if ("o", bt) not in tiles:
                tiles[("o", bt)] = outs.tile([P, K * S], F32, name="o_sb")
            eng.tensor_tensor(
                out=ks(tiles[("o", bt)][:, k0 * S:k1 * S], S)[:, :, sh * SH:(sh + 1) * SH],
                in0=ks(tiles[("dc", r)][:, k0 * SH:k1 * SH], SH),
                in1=ks(tiles[("rn", r)][:, k0 * SH:k1 * SH], SH),
                op=ALU.mult,
            )

        def fin(r, h):
            bt, sh = divmod(r, HALVES)
            if bt == NBT - 1:
                return
            fin_part(nc.vector, r, h * HALF_K, h * HALF_K + VECTOR_K)
            fin_part(nc.gpsimd, r, h * HALF_K + VECTOR_K, (h + 1) * HALF_K)
            if sh == HALVES - 1:
                cols = slice(h * HALF_K * S, (h + 1) * HALF_K * S)
                nc.sync.dma_start(out=out_flat[bt * P:(bt + 1) * P, cols], in_=tiles[("o", bt)][:, cols])

        def fin_last(r, kt):
            fin_part(nc.vector, r, kt * P, (kt + 1) * P)
            if r == ROUNDS - 1:
                cols = slice(kt * P * S, (kt + 1) * P * S)
                nc.sync.dma_start(
                    out=out_flat[(NBT - 1) * P:NBT * P, cols], in_=tiles[("o", NBT - 1)][:, cols]
                )

        for kt in range(NKT):
            transposes(("w", kt), unit(w_ld, kt))
        for kt in range(NKT):
            if kt % 2 == 0:
                copy_words(("w", kt), unit(w_raw, kt // 2), False)
                nc.vector.tensor_tensor(
                    out=unit(w_sq, kt), in0=unit(w_raw, kt // 2), in1=unit(w_raw, kt // 2), op=ALU.mult
                )
            else:
                square_bank(("w", kt), unit(w_sq, kt))
        transposes(("q", 0), unit(q_ld, 0))
        t_p(0, 0)
        t_p(0, 1)
        t_p(0, 2)
        q_copy(0)
        q_square(0)
        quantise(w_sq, w_codes, w_scales, 0, 2)
        quantise(w_sq, w_codes, w_scales, 2, 2)
        q_quantise(0)
        t_p(0, 3)
        sq(0, 0)
        sq(0, 1)
        pq(0, 0)
        pq(0, 1)
        t_p(1, 0)
        t_p(1, 1)
        q_norms(0)
        sq(0, 2)
        quant(0, 0)
        sq(0, 3)
        pq(0, 2)
        pq(0, 3)
        t_p(1, 2)
        t_p(1, 3)

        def period(r):
            nxt = r + 1 < ROUNDS
            bt = r // HALVES
            early_q = r % HALVES == 0 and bt + 1 < NBT
            late_q = r % HALVES == 1 and bt + 1 < NBT
            if nxt:
                sq(r + 1, 0)
                sq(r + 1, 1)
            if r == 0:
                q_factor(0)
            if nxt:
                sq(r + 1, 2)
            quant(r, 1)
            if late_q:
                q_square(bt + 1)
            if r > 0:
                fin(r - 1, 1)
            if nxt:
                pq(r + 1, 0)
                pq(r + 1, 1)
            else:
                fin_last(r - 1, 0)
            mx(r, 0)
            mx(r, 1)
            dc(r, 0)
            if not nxt:
                fin_last(r - 1, 1)
            dc(r, 1)
            rs(r, 0)
            if nxt:
                sq(r + 1, 3)
            rs(r, 1)
            if early_q:
                transposes(("q", bt + 1), unit(q_ld, bt + 1))
                q_copy(bt + 1)
            if nxt:
                quant(r + 1, 0)
            if late_q:
                q_quantise(bt + 1)
            fin(r, 0)
            if nxt:
                pq(r + 1, 2)
                pq(r + 1, 3)
            else:
                fin_last(r - 1, 2)
                fin_last(r, 0)
            mx(r, 2)
            mx(r, 3)
            dc(r, 2)
            if not nxt:
                fin_last(r - 1, 3)
                fin_last(r, 1)
            dc(r, 3)
            rs(r, 2)
            rs(r, 3)
            if not nxt:
                fin_last(r, 2)
                fin_last(r, 3)
            if late_q:
                q_norms(bt + 1)
                q_factor(bt + 1)
            if r + 2 < ROUNDS:
                for sl in range(SH):
                    t_p(r + 2, sl)

        for r in range(ROUNDS):
            period(r)
